import numpy as np
import ml_dtypes

BF16 = ml_dtypes.bfloat16


def bf(x):
    return np.asarray(x, np.float32).astype(BF16)


def f32(x):
    return np.asarray(x, np.float32)


def f64(x):
    return np.asarray(x).astype(np.float64)


def striped(idx):
    return np.tile(idx.reshape(-1, 16).T, (8, 1))


D, V, B, T, N = 128, 2048, 128, 32, 4096
LN_EPS = 1e-5


def setup_inputs():
    table = f32(bf(0.4 * np.random.standard_normal((D, V)) + 0.2 * np.random.standard_normal((D, 1))))
    kpos = bf(np.random.standard_normal((D, T)))
    qpos = bf(np.random.standard_normal((D, 1)))
    gain = f32(1.0 + 0.1 * np.random.standard_normal((D, 1)))
    shift = f32(0.1 * np.random.standard_normal((D, 1)))
    return {"table": table, "kpos": kpos, "qpos": qpos, "gain": gain, "shift": shift, "offs": striped(np.random.permutation(np.tile(np.arange(V), 2))[:N])}


def reference(table, kpos, qpos, gain, shift, offs):
    idx = offs[:16].T.reshape(-1)
    tb = f64(table)
    mu = tb.sum(axis=1, keepdims=True) / V
    sc = (f64(qpos) * f64(kpos)).sum(axis=0) / np.sqrt(D)
    a = np.exp(sc - sc.max())
    a = a / a.sum()
    err = tb[:, idx] - mu
    f = (err.reshape(D, B, T) * a).sum(axis=2)
    m = f.mean(axis=0, keepdims=True)
    var = ((f - m) ** 2).mean(axis=0, keepdims=True)
    fn = (f - m) / np.sqrt(var + LN_EPS) * f64(gain) + f64(shift)
    return fn.T @ tb

@@ -1,0 +1,126 @@
+import math
+
+import concourse.mybir as mybir
+from concourse.masks import make_identity
+
+F32 = mybir.dt.float32
+BF16 = mybir.dt.bfloat16
+U16 = mybir.dt.uint16
+ALU = mybir.AluOpType
+ACT = mybir.ActivationFunctionType
+X = mybir.AxisListType.X
+
+D, V, B, T, N = 128, 2048, 128, 32, 4096
+LN_EPS = 1e-5
+BANK = 512
+PIECE = 512
+SEQS = PIECE // T
+
+FLOPS = 2 * B * D * V + 2 * D * N
+
+
+def tile_gdtransformer_kernel(tc, table, kpos, qpos, gain, shift, offs, out):
+    nc = tc.nc
+    with (
+        tc.tile_pool(name="held", bufs=1) as held,
+        tc.tile_pool(name="ring", bufs=2) as ring,
+        tc.psum_pool(name="psum", bufs=1) as psum,
+        tc.psum_pool(name="logits", bufs=4) as logits,
+    ):
+        offsets = held.tile([D, N // 16], U16, name="offsets")
+        nc.sync.dma_start(offsets[:], offs)
+        table_sb = held.tile([D, V], F32, name="table_sb")
+        for i in range(V // BANK):
+            queue = nc.scalar if i % 2 == 0 else nc.sync
+            queue.dma_start(table_sb[:, i * BANK : (i + 1) * BANK], table[:, i * BANK : (i + 1) * BANK])
+        kpos_sb = held.tile([D, T], BF16, name="kpos_sb")
+        nc.scalar.dma_start(kpos_sb[:], kpos)
+        qpos_sb = held.tile([D, 1], BF16, name="qpos_sb")
+        nc.sync.dma_start(qpos_sb[:], qpos)
+        gain_sb = held.tile([D, 1], F32, name="gain_sb")
+        nc.scalar.dma_start(gain_sb[:], gain)
+        shift_sb = held.tile([D, 1], F32, name="shift_sb")
+        nc.sync.dma_start(shift_sb[:], shift)
+
+        mean_mat = held.tile([D, D], F32, name="mean_mat")
+        nc.vector.memset(mean_mat[:], 1.0 / D)
+        identity = held.tile([D, D], F32, name="identity")
+        make_identity(nc, identity[:])
+        center_mat = held.tile([D, D], F32, name="center_mat")
+        nc.vector.tensor_scalar_add(center_mat[:], identity[:], -1.0 / D)
+        eps = held.tile([D, 1], F32, name="eps")
+        nc.vector.memset(eps[:], LN_EPS)
+
+        qk = held.tile([D, T], F32, name="qk")
+        nc.vector.tensor_scalar_mul(qk[:], kpos_sb[:], qpos_sb[:, 0:1])
+        score_ps = psum.tile([D, T], F32, name="score_ps")
+        nc.tensor.matmul(score_ps[:], mean_mat[:], qk[:], start=True, stop=True)
+        to_score = D / math.sqrt(D)
+        score_max = held.tile([D, 1], F32, name="score_max")
+        nc.vector.reduce_max(score_max[:], score_ps[:], axis=X)
+        minus_max = held.tile([D, 1], F32, name="minus_max")
+        nc.vector.tensor_scalar_mul(minus_max[:], score_max[:], -to_score)
+        expo = held.tile([D, T], F32, name="expo")
+        expo_sum = held.tile([D, 1], F32, name="expo_sum")
+        nc.scalar.activation(
+            expo[:], score_ps[:], ACT.Exp, bias=minus_max[:, 0:1], scale=to_score, accum_out=expo_sum[:, 0:1]
+        )
+        inv_sum = held.tile([D, 1], F32, name="inv_sum")
+        nc.vector.reciprocal(inv_sum[:], expo_sum[:])
+        attn = held.tile([D, T], F32, name="attn")
+        nc.vector.tensor_scalar_mul(attn[:], expo[:], inv_sum[:, 0:1])
+
+        table_bf = held.tile([D, V], BF16, name="table_bf")
+        chunk_sum = held.tile([D, V // BANK], F32, name="chunk_sum")
+        for i in range(V // BANK):
+            chunk = table_sb[:, i * BANK : (i + 1) * BANK]
+            nc.vector.reduce_sum(chunk_sum[:, i : i + 1], chunk, axis=X)
+            nc.scalar.copy(table_bf[:, i * BANK : (i + 1) * BANK], chunk)
+        table_sum = held.tile([D, 1], F32, name="table_sum")
+        nc.vector.reduce_sum(table_sum[:], chunk_sum[:], axis=X)
+        minus_mu = held.tile([D, PIECE], F32, name="minus_mu")
+        nc.vector.tensor_scalar_mul(minus_mu[:], table_sum[:, 0:1].to_broadcast([D, PIECE]), -1.0 / V)
+
+        pooled = held.tile([D, B], F32, name="pooled")
+        for g in range(N // PIECE):
+            err = ring.tile([D, PIECE], F32, name="err")
+            nc.vector.tensor_tensor(
+                err[:],
+                table_sb[:].indirect(offsets[:, g * (PIECE // 16) : (g + 1) * (PIECE // 16)]),
+                minus_mu[:],
+                ALU.add,
+            )
+            weighted = ring.tile([D, SEQS, T], F32, name="weighted")
+            nc.vector.tensor_tensor(
+                weighted[:],
+                err[:].rearrange("c (b t) -> c b t", t=T),
+                attn[:].unsqueeze(1).to_broadcast([D, SEQS, T]),
+                ALU.mult,
+            )
+            nc.vector.reduce_sum(pooled[:, g * SEQS : (g + 1) * SEQS], weighted[:], axis=X)
+
+        centered_ps = psum.tile([D, B], F32, name="centered_ps")
+        nc.tensor.matmul(centered_ps[:], center_mat[:], pooled[:], start=True, stop=True)
+        squared = held.tile([D, B], F32, name="squared")
+        nc.scalar.activation(squared[:], centered_ps[:], ACT.Square)
+        var_ps = psum.tile([D, B], F32, name="var_ps")
+        nc.tensor.matmul(var_ps[:], mean_mat[:], squared[:], start=True, stop=True)
+        std = held.tile([D, B], F32, name="std")
+        nc.scalar.activation(std[:], var_ps[:], ACT.Sqrt, bias=eps[:, 0:1])
+        inv_std = held.tile([D, B], F32, name="inv_std")
+        nc.vector.reciprocal(inv_std[:], std[:])
+        normed = held.tile([D, B], F32, name="normed")
+        nc.vector.tensor_tensor(normed[:], centered_ps[:], inv_std[:], ALU.mult)
+        fn = held.tile([D, B], BF16, name="fn")
+        nc.vector.tensor_scalar(fn[:], normed[:], gain_sb[:, 0:1], shift_sb[:, 0:1], ALU.mult, ALU.add)
+
+        for i in range(V // BANK):
+            logits_ps = logits.tile([B, BANK], F32, name="logits_ps")
+            nc.tensor.matmul(logits_ps[:], fn[:], table_bf[:, i * BANK : (i + 1) * BANK], start=True, stop=True)
+            logits_sb = ring.tile([B, BANK], F32, name="logits_sb")
+            if i % 2 == 0:
+                nc.vector.tensor_copy(logits_sb[:], logits_ps[:])
+                nc.sync.dma_start(out[:, i * BANK : (i + 1) * BANK], logits_sb[:])
+            else:
+                nc.scalar.copy(logits_sb[:], logits_ps[:])
+                nc.scalar.dma_start(out[:, i * BANK : (i + 1) * BANK], logits_sb[:])

@@ -14,7 +14,9 @@ D, V, B, T, N = 128, 2048, 128, 32, 4096
 LN_EPS = 1e-5
 BANK = 512
 PIECE = 512
-SEQS = PIECE // T
+BLOCK = 128
+BLOCKS = PIECE // BLOCK
+SEQS = BLOCK // T
 
 FLOPS = 2 * B * D * V + 2 * D * N
 
@@ -25,7 +27,7 @@ def tile_gdtransformer_kernel(tc, table, kpos, qpos, gain, shift, offs, out):
         tc.tile_pool(name="held", bufs=1) as held,
         tc.tile_pool(name="ring", bufs=2) as ring,
         tc.psum_pool(name="psum", bufs=1) as psum,
-        tc.psum_pool(name="logits", bufs=4) as logits,
+        tc.psum_pool(name="banks", bufs=4) as banks,
     ):
         offsets = held.tile([D, N // 16], U16, name="offsets")
         nc.sync.dma_start(offsets[:], offs)
@@ -81,7 +83,17 @@ def tile_gdtransformer_kernel(tc, table, kpos, qpos, gain, shift, offs, out):
         minus_mu = held.tile([D, PIECE], F32, name="minus_mu")
         nc.vector.tensor_scalar_mul(minus_mu[:], table_sum[:, 0:1].to_broadcast([D, PIECE]), -1.0 / V)
 
-        pooled = held.tile([D, B], F32, name="pooled")
+        masked = held.tile([BLOCK, SEQS, T], F32, name="masked")
+        nc.vector.tensor_tensor(
+            masked[:],
+            identity[:].rearrange("j (s t) -> j s t", t=T),
+            attn[:].unsqueeze(1).to_broadcast([BLOCK, SEQS, T]),
+            ALU.mult,
+        )
+        pool_mat = held.tile([BLOCK, SEQS], F32, name="pool_mat")
+        nc.vector.reduce_sum(pool_mat[:], masked[:], axis=X)
+
+        pooled_ps = psum.tile([D, B], F32, name="pooled_ps")
         for g in range(N // PIECE):
             err = ring.tile([D, PIECE], F32, name="err")
             nc.vector.tensor_tensor(
@@ -90,14 +102,18 @@ def tile_gdtransformer_kernel(tc, table, kpos, qpos, gain, shift, offs, out):
                 minus_mu[:],
                 ALU.add,
             )
-            weighted = ring.tile([D, SEQS, T], F32, name="weighted")
-            nc.vector.tensor_tensor(
-                weighted[:],
-                err[:].rearrange("c (b t) -> c b t", t=T),
-                attn[:].unsqueeze(1).to_broadcast([D, SEQS, T]),
-                ALU.mult,
-            )
-            nc.vector.reduce_sum(pooled[:, g * SEQS : (g + 1) * SEQS], weighted[:], axis=X)
+            flipped_ps = banks.tile([BLOCK, BLOCKS * D], F32, name="flipped_ps", tag="bank")
+            for i in range(BLOCKS):
+                nc.tensor.transpose(flipped_ps[:, i * D : (i + 1) * D], err[:, i * BLOCK : (i + 1) * BLOCK], identity[:])
+            flipped = ring.tile([BLOCK, BLOCKS * D], F32, name="flipped")
+            nc.scalar.copy(flipped[:], flipped_ps[:])
+            for i in range(BLOCKS):
+                first = (g * BLOCKS + i) * SEQS
+                nc.tensor.matmul(
+                    pooled_ps[:, first : first + SEQS], flipped[:, i * D : (i + 1) * D], pool_mat[:], start=True, stop=True
+                )
+        pooled = held.tile([D, B], F32, name="pooled")
+        nc.vector.tensor_copy(pooled[:], pooled_ps[:])
 
         centered_ps = psum.tile([D, B], F32, name="centered_ps")
         nc.tensor.matmul(centered_ps[:], center_mat[:], pooled[:], start=True, stop=True)
@@ -115,7 +131,7 @@ def tile_gdtransformer_kernel(tc, table, kpos, qpos, gain, shift, offs, out):
         nc.vector.tensor_scalar(fn[:], normed[:], gain_sb[:, 0:1], shift_sb[:, 0:1], ALU.mult, ALU.add)
 
         for i in range(V // BANK):
-            logits_ps = logits.tile([B, BANK], F32, name="logits_ps")
+            logits_ps = banks.tile([B, BANK], F32, name="logits_ps", tag="bank")
             nc.tensor.matmul(logits_ps[:], fn[:], table_bf[:, i * BANK : (i + 1) * BANK], start=True, stop=True)
             logits_sb = ring.tile([B, BANK], F32, name="logits_sb")
             if i % 2 == 0:

@@ -17,6 +17,7 @@ PIECE = 512
 BLOCK = 128
 BLOCKS = PIECE // BLOCK
 SEQS = BLOCK // T
+HALF = 64
 
 FLOPS = 2 * B * D * V + 2 * D * N
 
@@ -26,6 +27,7 @@ def tile_gdtransformer_kernel(tc, table, kpos, qpos, gain, shift, offs, out):
     with (
         tc.tile_pool(name="held", bufs=1) as held,
         tc.tile_pool(name="ring", bufs=2) as ring,
+        tc.tile_pool(name="flow", bufs=3) as flow,
         tc.psum_pool(name="psum", bufs=1) as psum,
         tc.psum_pool(name="banks", bufs=4) as banks,
     ):
@@ -90,12 +92,14 @@ def tile_gdtransformer_kernel(tc, table, kpos, qpos, gain, shift, offs, out):
             attn[:].unsqueeze(1).to_broadcast([BLOCK, SEQS, T]),
             ALU.mult,
         )
-        pool_mat = held.tile([BLOCK, SEQS], F32, name="pool_mat")
-        nc.vector.reduce_sum(pool_mat[:], masked[:], axis=X)
+        pool_band = held.tile([BLOCK, 2 * HALF - SEQS], F32, name="pool_band")
+        nc.gpsimd.memset(pool_band[:], 0.0)
+        nc.vector.reduce_sum(pool_band[:, HALF - SEQS : HALF], masked[:], axis=X)
 
         pooled_ps = psum.tile([D, B], F32, name="pooled_ps")
-        for g in range(N // PIECE):
-            err = ring.tile([D, PIECE], F32, name="err")
+
+        def look_up_and_flip(g):
+            err = flow.tile([D, PIECE], F32, name="err")
             nc.vector.tensor_tensor(
                 err[:],
                 table_sb[:].indirect(offsets[:, g * (PIECE // 16) : (g + 1) * (PIECE // 16)]),
@@ -105,13 +109,28 @@ def tile_gdtransformer_kernel(tc, table, kpos, qpos, gain, shift, offs, out):
             flipped_ps = banks.tile([BLOCK, BLOCKS * D], F32, name="flipped_ps", tag="bank")
             for i in range(BLOCKS):
                 nc.tensor.transpose(flipped_ps[:, i * D : (i + 1) * D], err[:, i * BLOCK : (i + 1) * BLOCK], identity[:])
-            flipped = ring.tile([BLOCK, BLOCKS * D], F32, name="flipped")
+            flipped = flow.tile([BLOCK, BLOCKS * D], F32, name="flipped")
             nc.scalar.copy(flipped[:], flipped_ps[:])
+            return flipped
+
+        def pool(g, flipped):
             for i in range(BLOCKS):
-                first = (g * BLOCKS + i) * SEQS
+                group, place = divmod((g * BLOCKS + i) * SEQS, HALF)
                 nc.tensor.matmul(
-                    pooled_ps[:, first : first + SEQS], flipped[:, i * D : (i + 1) * D], pool_mat[:], start=True, stop=True
+                    pooled_ps[:, group * HALF : (group + 1) * HALF],
+                    flipped[:, i * D : (i + 1) * D],
+                    pool_band[:, HALF - SEQS - place : 2 * HALF - SEQS - place],
+                    start=(place == 0),
+                    stop=(place == HALF - SEQS),
                 )
+
+        pieces = N // PIECE
+        waiting = look_up_and_flip(0)
+        for g in range(1, pieces):
+            flipped = look_up_and_flip(g)
+            pool(g - 1, waiting)
+            waiting = flipped
+        pool(pieces - 1, waiting)
         pooled = held.tile([D, B], F32, name="pooled")
         nc.vector.tensor_copy(pooled[:], pooled_ps[:])
 

@@ -14,10 +14,7 @@ D, V, B, T, N = 128, 2048, 128, 32, 4096
 LN_EPS = 1e-5
 BANK = 512
 PIECE = 512
-BLOCK = 128
-BLOCKS = PIECE // BLOCK
-SEQS = BLOCK // T
-HALF = 64
+SEQS = PIECE // T
 
 FLOPS = 2 * B * D * V + 2 * D * N
 
@@ -29,7 +26,7 @@ def tile_gdtransformer_kernel(tc, table, kpos, qpos, gain, shift, offs, out):
         tc.tile_pool(name="ring", bufs=2) as ring,
         tc.tile_pool(name="flow", bufs=3) as flow,
         tc.psum_pool(name="psum", bufs=1) as psum,
-        tc.psum_pool(name="banks", bufs=4) as banks,
+        tc.psum_pool(name="logits", bufs=4) as logits,
     ):
         offsets = held.tile([D, N // 16], U16, name="offsets")
         nc.sync.dma_start(offsets[:], offs)
@@ -85,20 +82,9 @@ def tile_gdtransformer_kernel(tc, table, kpos, qpos, gain, shift, offs, out):
         minus_mu = held.tile([D, PIECE], F32, name="minus_mu")
         nc.vector.tensor_scalar_mul(minus_mu[:], table_sum[:, 0:1].to_broadcast([D, PIECE]), -1.0 / V)
 
-        masked = held.tile([BLOCK, SEQS, T], F32, name="masked")
-        nc.vector.tensor_tensor(
-            masked[:],
-            identity[:].rearrange("j (s t) -> j s t", t=T),
-            attn[:].unsqueeze(1).to_broadcast([BLOCK, SEQS, T]),
-            ALU.mult,
-        )
-        pool_band = held.tile([BLOCK, 2 * HALF - SEQS], F32, name="pool_band")
-        nc.gpsimd.memset(pool_band[:], 0.0)
-        nc.vector.reduce_sum(pool_band[:, HALF - SEQS : HALF], masked[:], axis=X)
+        pooled = held.tile([D, B], F32, name="pooled")
 
-        pooled_ps = psum.tile([D, B], F32, name="pooled_ps")
-
-        def look_up_and_flip(g):
+        def look_up_and_weigh(g):
             err = flow.tile([D, PIECE], F32, name="err")
             nc.vector.tensor_tensor(
                 err[:],
@@ -106,33 +92,22 @@ def tile_gdtransformer_kernel(tc, table, kpos, qpos, gain, shift, offs, out):
                 minus_mu[:],
                 ALU.add,
             )
-            flipped_ps = banks.tile([BLOCK, BLOCKS * D], F32, name="flipped_ps", tag="bank")
-            for i in range(BLOCKS):
-                nc.tensor.transpose(flipped_ps[:, i * D : (i + 1) * D], err[:, i * BLOCK : (i + 1) * BLOCK], identity[:])
-            flipped = flow.tile([BLOCK, BLOCKS * D], F32, name="flipped")
-            nc.scalar.copy(flipped[:], flipped_ps[:])
-            return flipped
-
-        def pool(g, flipped):
-            for i in range(BLOCKS):
-                group, place = divmod((g * BLOCKS + i) * SEQS, HALF)
-                nc.tensor.matmul(
-                    pooled_ps[:, group * HALF : (group + 1) * HALF],
-                    flipped[:, i * D : (i + 1) * D],
-                    pool_band[:, HALF - SEQS - place : 2 * HALF - SEQS - place],
-                    start=(place == 0),
-                    stop=(place == HALF - SEQS),
-                )
+            weighted = flow.tile([D, SEQS, T], F32, name="weighted")
+            nc.gpsimd.tensor_tensor(
+                weighted[:],
+                err[:].rearrange("c (b t) -> c b t", t=T),
+                attn[:].unsqueeze(1).to_broadcast([D, SEQS, T]),
+                ALU.mult,
+            )
+            return weighted
 
         pieces = N // PIECE
-        waiting = look_up_and_flip(0)
+        waiting = look_up_and_weigh(0)
         for g in range(1, pieces):
-            flipped = look_up_and_flip(g)
-            pool(g - 1, waiting)
-            waiting = flipped
-        pool(pieces - 1, waiting)
-        pooled = held.tile([D, B], F32, name="pooled")
-        nc.vector.tensor_copy(pooled[:], pooled_ps[:])
+            weighted = look_up_and_weigh(g)
+            nc.vector.reduce_sum(pooled[:, (g - 1) * SEQS : g * SEQS], waiting[:], axis=X)
+            waiting = weighted
+        nc.vector.reduce_sum(pooled[:, (pieces - 1) * SEQS : pieces * SEQS], waiting[:], axis=X)
 
         centered_ps = psum.tile([D, B], F32, name="centered_ps")
         nc.tensor.matmul(centered_ps[:], center_mat[:], pooled[:], start=True, stop=True)
@@ -150,7 +125,7 @@ def tile_gdtransformer_kernel(tc, table, kpos, qpos, gain, shift, offs, out):
         nc.vector.tensor_scalar(fn[:], normed[:], gain_sb[:, 0:1], shift_sb[:, 0:1], ALU.mult, ALU.add)
 
         for i in range(V // BANK):
-            logits_ps = banks.tile([B, BANK], F32, name="logits_ps", tag="bank")
+            logits_ps = logits.tile([B, BANK], F32, name="logits_ps")
             nc.tensor.matmul(logits_ps[:], fn[:], table_bf[:, i * BANK : (i + 1) * BANK], start=True, stop=True)
             logits_sb = ring.tile([B, BANK], F32, name="logits_sb")
             if i % 2 == 0:

@@ -14,7 +14,10 @@ D, V, B, T, N = 128, 2048, 128, 32, 4096
 LN_EPS = 1e-5
 BANK = 512
 PIECE = 512
-SEQS = PIECE // T
+BLOCK = 128
+BLOCKS = PIECE // BLOCK
+SEQS = BLOCK // T
+HALF = B // 2
 
 FLOPS = 2 * B * D * V + 2 * D * N
 
@@ -23,10 +26,9 @@ def tile_gdtransformer_kernel(tc, table, kpos, qpos, gain, shift, offs, out):
     nc = tc.nc
     with (
         tc.tile_pool(name="held", bufs=1) as held,
-        tc.tile_pool(name="ring", bufs=2) as ring,
-        tc.tile_pool(name="flow", bufs=3) as flow,
+        tc.tile_pool(name="flow", bufs=4) as flow,
         tc.psum_pool(name="psum", bufs=1) as psum,
-        tc.psum_pool(name="logits", bufs=4) as logits,
+        tc.psum_pool(name="banks", bufs=4) as banks,
     ):
         offsets = held.tile([D, N // 16], U16, name="offsets")
         nc.sync.dma_start(offsets[:], offs)
@@ -70,6 +72,8 @@ def tile_gdtransformer_kernel(tc, table, kpos, qpos, gain, shift, offs, out):
         nc.vector.reciprocal(inv_sum[:], expo_sum[:])
         attn = held.tile([D, T], F32, name="attn")
         nc.vector.tensor_scalar_mul(attn[:], expo[:], inv_sum[:, 0:1])
+        table_change = held.tile([D, 1], F32, name="table_change")
+        nc.scalar.activation(table_change[:], expo_sum[:], ACT.Sqrt)
 
         table_bf = held.tile([D, V], BF16, name="table_bf")
         chunk_sum = held.tile([D, V // BANK], F32, name="chunk_sum")
@@ -82,9 +86,20 @@ def tile_gdtransformer_kernel(tc, table, kpos, qpos, gain, shift, offs, out):
         minus_mu = held.tile([D, PIECE], F32, name="minus_mu")
         nc.vector.tensor_scalar_mul(minus_mu[:], table_sum[:, 0:1].to_broadcast([D, PIECE]), -1.0 / V)
 
+        masked = held.tile([BLOCK, SEQS, T], F32, name="masked")
+        nc.vector.tensor_tensor(
+            masked[:],
+            identity[:].rearrange("j (s t) -> j s t", t=T),
+            attn[:].unsqueeze(1).to_broadcast([BLOCK, SEQS, T]),
+            ALU.mult,
+        )
+        pool_band = held.tile([BLOCK, 2 * HALF - SEQS], F32, name="pool_band")
+        nc.gpsimd.memset(pool_band[:], 0.0)
+        nc.vector.reduce_sum(pool_band[:, HALF - SEQS : HALF], masked[:], axis=X)
+
         pooled = held.tile([D, B], F32, name="pooled")
 
-        def look_up_and_weigh(g):
+        def look_up(g):
             err = flow.tile([D, PIECE], F32, name="err")
             nc.vector.tensor_tensor(
                 err[:],
@@ -92,22 +107,48 @@ def tile_gdtransformer_kernel(tc, table, kpos, qpos, gain, shift, offs, out):
                 minus_mu[:],
                 ALU.add,
             )
-            weighted = flow.tile([D, SEQS, T], F32, name="weighted")
-            nc.gpsimd.tensor_tensor(
+            return err
+
+        def flip(err):
+            flipped_ps = banks.tile([BLOCK, BLOCKS * D], F32, name="flipped_ps", tag="bank")
+            for i in range(BLOCKS):
+                nc.tensor.transpose(flipped_ps[:, i * D : (i + 1) * D], err[:, i * BLOCK : (i + 1) * BLOCK], identity[:])
+            flipped = flow.tile([BLOCK, BLOCKS * D], F32, name="flipped")
+            nc.scalar.copy(flipped[:], flipped_ps[:])
+            return flipped
+
+        pooled_ps = psum.tile([D, HALF], F32, name="pooled_ps")
+
+        def contract(g, flipped):
+            for i in range(BLOCKS):
+                place = (g * BLOCKS + i) * SEQS
+                nc.tensor.matmul(
+                    pooled_ps[:],
+                    flipped[:, i * D : (i + 1) * D],
+                    pool_band[:, HALF - SEQS - place : 2 * HALF - SEQS - place],
+                    start=(place == 0),
+                    stop=(place == HALF - SEQS),
+                )
+
+        tensor_pieces = HALF * T // PIECE
+        waiting = flip(look_up(0))
+        for g in range(1, tensor_pieces):
+            flipped = flip(look_up(g))
+            contract(g - 1, waiting)
+            waiting = flipped
+        contract(tensor_pieces - 1, waiting)
+
+        for g in range(tensor_pieces, N // PIECE):
+            err = look_up(g)
+            weighted = flow.tile([D, PIECE // T, T], F32, name="weighted")
+            nc.vector.tensor_tensor(
                 weighted[:],
                 err[:].rearrange("c (b t) -> c b t", t=T),
-                attn[:].unsqueeze(1).to_broadcast([D, SEQS, T]),
+                attn[:].unsqueeze(1).to_broadcast([D, PIECE // T, T]),
                 ALU.mult,
             )
-            return weighted
-
-        pieces = N // PIECE
-        waiting = look_up_and_weigh(0)
-        for g in range(1, pieces):
-            weighted = look_up_and_weigh(g)
-            nc.vector.reduce_sum(pooled[:, (g - 1) * SEQS : g * SEQS], waiting[:], axis=X)
-            waiting = weighted
-        nc.vector.reduce_sum(pooled[:, (pieces - 1) * SEQS : pieces * SEQS], waiting[:], axis=X)
+            nc.vector.reduce_sum(pooled[:, g * (PIECE // T) : (g + 1) * (PIECE // T)], weighted[:], axis=X)
+        nc.vector.tensor_copy(pooled[:, 0:HALF], pooled_ps[:])
 
         centered_ps = psum.tile([D, B], F32, name="centered_ps")
         nc.tensor.matmul(centered_ps[:], center_mat[:], pooled[:], start=True, stop=True)
@@ -124,13 +165,14 @@ def tile_gdtransformer_kernel(tc, table, kpos, qpos, gain, shift, offs, out):
         fn = held.tile([D, B], BF16, name="fn")
         nc.vector.tensor_scalar(fn[:], normed[:], gain_sb[:, 0:1], shift_sb[:, 0:1], ALU.mult, ALU.add)
 
+        logits_sb = held.tile([B, V], F32, name="logits_sb")
         for i in range(V // BANK):
-            logits_ps = logits.tile([B, BANK], F32, name="logits_ps")
-            nc.tensor.matmul(logits_ps[:], fn[:], table_bf[:, i * BANK : (i + 1) * BANK], start=True, stop=True)
-            logits_sb = ring.tile([B, BANK], F32, name="logits_sb")
+            words = slice(i * BANK, (i + 1) * BANK)
+            logits_ps = banks.tile([B, BANK], F32, name="logits_ps", tag="bank")
+            nc.tensor.matmul(logits_ps[:], fn[:], table_bf[:, words], start=True, stop=True)
             if i % 2 == 0:
-                nc.vector.tensor_copy(logits_sb[:], logits_ps[:])
-                nc.sync.dma_start(out[:, i * BANK : (i + 1) * BANK], logits_sb[:])
+                nc.vector.tensor_copy(logits_sb[:, words], logits_ps[:])
+                nc.sync.dma_start(out[:, words], logits_sb[:, words])
             else:
-                nc.scalar.copy(logits_sb[:], logits_ps[:])
-                nc.scalar.dma_start(out[:, i * BANK : (i + 1) * BANK], logits_sb[:])
+                nc.scalar.copy(logits_sb[:, words], logits_ps[:])
+                nc.scalar.dma_start(out[:, words], logits_sb[:, words])

@@ -17,7 +17,8 @@ PIECE = 512
 BLOCK = 128
 BLOCKS = PIECE // BLOCK
 SEQS = BLOCK // T
-HALF = B // 2
+GROUP = 64
+TENSOR_PIECES = 6
 
 FLOPS = 2 * B * D * V + 2 * D * N
 
@@ -73,7 +74,7 @@ def tile_gdtransformer_kernel(tc, table, kpos, qpos, gain, shift, offs, out):
         attn = held.tile([D, T], F32, name="attn")
         nc.vector.tensor_scalar_mul(attn[:], expo[:], inv_sum[:, 0:1])
         table_change = held.tile([D, 1], F32, name="table_change")
-        nc.scalar.activation(table_change[:], expo_sum[:], ACT.Sqrt)
+        nc.scalar.activation(table_change[:], expo_sum[:], ACT.Abs_reciprocal_sqrt)
 
         table_bf = held.tile([D, V], BF16, name="table_bf")
         chunk_sum = held.tile([D, V // BANK], F32, name="chunk_sum")
@@ -93,9 +94,9 @@ def tile_gdtransformer_kernel(tc, table, kpos, qpos, gain, shift, offs, out):
             attn[:].unsqueeze(1).to_broadcast([BLOCK, SEQS, T]),
             ALU.mult,
         )
-        pool_band = held.tile([BLOCK, 2 * HALF - SEQS], F32, name="pool_band")
+        pool_band = held.tile([BLOCK, 2 * GROUP - SEQS], F32, name="pool_band")
         nc.gpsimd.memset(pool_band[:], 0.0)
-        nc.vector.reduce_sum(pool_band[:, HALF - SEQS : HALF], masked[:], axis=X)
+        nc.vector.reduce_sum(pool_band[:, GROUP - SEQS : GROUP], masked[:], axis=X)
 
         pooled = held.tile([D, B], F32, name="pooled")
 
@@ -117,28 +118,30 @@ def tile_gdtransformer_kernel(tc, table, kpos, qpos, gain, shift, offs, out):
             nc.scalar.copy(flipped[:], flipped_ps[:])
             return flipped
 
-        pooled_ps = psum.tile([D, HALF], F32, name="pooled_ps")
+        pooled_ps = psum.tile([D, B], F32, name="pooled_ps")
 
         def contract(g, flipped):
             for i in range(BLOCKS):
-                place = (g * BLOCKS + i) * SEQS
+                block = g * BLOCKS + i
+                group, place = divmod(block * SEQS, GROUP)
                 nc.tensor.matmul(
-                    pooled_ps[:],
+                    pooled_ps[:, group * GROUP : (group + 1) * GROUP],
                     flipped[:, i * D : (i + 1) * D],
-                    pool_band[:, HALF - SEQS - place : 2 * HALF - SEQS - place],
+                    pool_band[:, GROUP - SEQS - place : 2 * GROUP - SEQS - place],
                     start=(place == 0),
-                    stop=(place == HALF - SEQS),
+                    stop=(place == GROUP - SEQS or block == TENSOR_PIECES * BLOCKS - 1),
                 )
 
-        tensor_pieces = HALF * T // PIECE
         waiting = flip(look_up(0))
-        for g in range(1, tensor_pieces):
+        for g in range(1, TENSOR_PIECES):
             flipped = flip(look_up(g))
             contract(g - 1, waiting)
             waiting = flipped
-        contract(tensor_pieces - 1, waiting)
+        contract(TENSOR_PIECES - 1, waiting)
+        tensor_seqs = TENSOR_PIECES * PIECE // T
+        nc.scalar.copy(pooled[:, 0:tensor_seqs], pooled_ps[:, 0:tensor_seqs])
 
-        for g in range(tensor_pieces, N // PIECE):
+        for g in range(TENSOR_PIECES, N // PIECE):
             err = look_up(g)
             weighted = flow.tile([D, PIECE // T, T], F32, name="weighted")
             nc.vector.tensor_tensor(
@@ -148,7 +151,6 @@ def tile_gdtransformer_kernel(tc, table, kpos, qpos, gain, shift, offs, out):
                 ALU.mult,
             )
             nc.vector.reduce_sum(pooled[:, g * (PIECE // T) : (g + 1) * (PIECE // T)], weighted[:], axis=X)
-        nc.vector.tensor_copy(pooled[:, 0:HALF], pooled_ps[:])
 
         centered_ps = psum.tile([D, B], F32, name="centered_ps")
         nc.tensor.matmul(centered_ps[:], center_mat[:], pooled[:], start=True, stop=True)
@@ -156,10 +158,8 @@ def tile_gdtransformer_kernel(tc, table, kpos, qpos, gain, shift, offs, out):
         nc.scalar.activation(squared[:], centered_ps[:], ACT.Square)
         var_ps = psum.tile([D, B], F32, name="var_ps")
         nc.tensor.matmul(var_ps[:], mean_mat[:], squared[:], start=True, stop=True)
-        std = held.tile([D, B], F32, name="std")
-        nc.scalar.activation(std[:], var_ps[:], ACT.Sqrt, bias=eps[:, 0:1])
         inv_std = held.tile([D, B], F32, name="inv_std")
-        nc.vector.reciprocal(inv_std[:], std[:])
+        nc.scalar.activation(inv_std[:], var_ps[:], ACT.Abs_reciprocal_sqrt, bias=eps[:, 0:1])
         normed = held.tile([D, B], F32, name="normed")
         nc.vector.tensor_tensor(normed[:], centered_ps[:], inv_std[:], ALU.mult)
         fn = held.tile([D, B], BF16, name="fn")

@@ -18,7 +18,7 @@ BLOCK = 128
 BLOCKS = PIECE // BLOCK
 SEQS = BLOCK // T
 GROUP = 64
-TENSOR_PIECES = 6
+TENSOR_PIECES = 5
 
 FLOPS = 2 * B * D * V + 2 * D * N
 

@@ -14,11 +14,15 @@ D, V, B, T, N = 128, 2048, 128, 32, 4096
 LN_EPS = 1e-5
 BANK = 512
 PIECE = 512
+PIECES = N // PIECE
+LOOK_UPS = (1, 2, 2, 2, 1)
+assert sum(LOOK_UPS) == PIECES
+WIDEST = max(LOOK_UPS) * PIECE
 BLOCK = 128
 BLOCKS = PIECE // BLOCK
 SEQS = BLOCK // T
-GROUP = 64
-TENSOR_PIECES = 5
+STRIP = 32
+assert BLOCKS * STRIP == B and PIECES * SEQS == STRIP
 
 FLOPS = 2 * B * D * V + 2 * D * N
 
@@ -31,16 +35,16 @@ def tile_gdtransformer_kernel(tc, table, kpos, qpos, gain, shift, offs, out):
         tc.psum_pool(name="psum", bufs=1) as psum,
         tc.psum_pool(name="banks", bufs=4) as banks,
     ):
+        kpos_sb = held.tile([D, T], BF16, name="kpos_sb")
+        nc.scalar.dma_start(kpos_sb[:], kpos)
+        qpos_sb = held.tile([D, 1], BF16, name="qpos_sb")
+        nc.sync.dma_start(qpos_sb[:], qpos)
         offsets = held.tile([D, N // 16], U16, name="offsets")
         nc.sync.dma_start(offsets[:], offs)
         table_sb = held.tile([D, V], F32, name="table_sb")
         for i in range(V // BANK):
             queue = nc.scalar if i % 2 == 0 else nc.sync
             queue.dma_start(table_sb[:, i * BANK : (i + 1) * BANK], table[:, i * BANK : (i + 1) * BANK])
-        kpos_sb = held.tile([D, T], BF16, name="kpos_sb")
-        nc.scalar.dma_start(kpos_sb[:], kpos)
-        qpos_sb = held.tile([D, 1], BF16, name="qpos_sb")
-        nc.sync.dma_start(qpos_sb[:], qpos)
         gain_sb = held.tile([D, 1], F32, name="gain_sb")
         nc.scalar.dma_start(gain_sb[:], gain)
         shift_sb = held.tile([D, 1], F32, name="shift_sb")
@@ -50,8 +54,6 @@ def tile_gdtransformer_kernel(tc, table, kpos, qpos, gain, shift, offs, out):
         nc.vector.memset(mean_mat[:], 1.0 / D)
         identity = held.tile([D, D], F32, name="identity")
         make_identity(nc, identity[:])
-        center_mat = held.tile([D, D], F32, name="center_mat")
-        nc.vector.tensor_scalar_add(center_mat[:], identity[:], -1.0 / D)
         eps = held.tile([D, 1], F32, name="eps")
         nc.vector.memset(eps[:], LN_EPS)
 
@@ -84,8 +86,9 @@ def tile_gdtransformer_kernel(tc, table, kpos, qpos, gain, shift, offs, out):
             nc.scalar.copy(table_bf[:, i * BANK : (i + 1) * BANK], chunk)
         table_sum = held.tile([D, 1], F32, name="table_sum")
         nc.vector.reduce_sum(table_sum[:], chunk_sum[:], axis=X)
-        minus_mu = held.tile([D, PIECE], F32, name="minus_mu")
-        nc.vector.tensor_scalar_mul(minus_mu[:], table_sum[:, 0:1].to_broadcast([D, PIECE]), -1.0 / V)
+        minus_mu = held.tile([D, WIDEST], F32, name="minus_mu")
+        nc.vector.tensor_scalar_mul(minus_mu[:, 0:PIECE], table_sum[:, 0:1].to_broadcast([D, PIECE]), -1.0 / V)
+        nc.scalar.copy(minus_mu[:, PIECE:WIDEST], minus_mu[:, 0:PIECE])
 
         masked = held.tile([BLOCK, SEQS, T], F32, name="masked")
         nc.vector.tensor_tensor(
@@ -94,76 +97,73 @@ def tile_gdtransformer_kernel(tc, table, kpos, qpos, gain, shift, offs, out):
             attn[:].unsqueeze(1).to_broadcast([BLOCK, SEQS, T]),
             ALU.mult,
         )
-        pool_band = held.tile([BLOCK, 2 * GROUP - SEQS], F32, name="pool_band")
+        pool_band = held.tile([BLOCK, 2 * STRIP - SEQS], F32, name="pool_band")
         nc.gpsimd.memset(pool_band[:], 0.0)
-        nc.vector.reduce_sum(pool_band[:, GROUP - SEQS : GROUP], masked[:], axis=X)
+        nc.vector.reduce_sum(pool_band[:, STRIP - SEQS : STRIP], masked[:], axis=X)
 
-        pooled = held.tile([D, B], F32, name="pooled")
-
-        def look_up(g):
-            err = flow.tile([D, PIECE], F32, name="err")
+        def look_up(g, pieces):
+            err = flow.tile([D, WIDEST], F32, name="err")
             nc.vector.tensor_tensor(
-                err[:],
-                table_sb[:].indirect(offsets[:, g * (PIECE // 16) : (g + 1) * (PIECE // 16)]),
-                minus_mu[:],
+                err[:, 0 : pieces * PIECE],
+                table_sb[:].indirect(offsets[:, g * (PIECE // 16) : (g + pieces) * (PIECE // 16)]),
+                minus_mu[:, 0 : pieces * PIECE],
                 ALU.add,
             )
             return err
 
-        def flip(err):
+        def flip(err, place):
             flipped_ps = banks.tile([BLOCK, BLOCKS * D], F32, name="flipped_ps", tag="bank")
             for i in range(BLOCKS):
-                nc.tensor.transpose(flipped_ps[:, i * D : (i + 1) * D], err[:, i * BLOCK : (i + 1) * BLOCK], identity[:])
+                first = place * PIECE + i * BLOCK
+                nc.tensor.transpose(flipped_ps[:, i * D : (i + 1) * D], err[:, first : first + BLOCK], identity[:])
             flipped = flow.tile([BLOCK, BLOCKS * D], F32, name="flipped")
             nc.scalar.copy(flipped[:], flipped_ps[:])
             return flipped
 
-        pooled_ps = psum.tile([D, B], F32, name="pooled_ps")
+        pooled_ps = psum.tile([B, D], F32, name="pooled_ps")
 
         def contract(g, flipped):
+            window = STRIP - SEQS - g * SEQS
             for i in range(BLOCKS):
-                block = g * BLOCKS + i
-                group, place = divmod(block * SEQS, GROUP)
                 nc.tensor.matmul(
-                    pooled_ps[:, group * GROUP : (group + 1) * GROUP],
+                    pooled_ps[i * STRIP : (i + 1) * STRIP, :],
+                    pool_band[:, window : window + STRIP],
                     flipped[:, i * D : (i + 1) * D],
-                    pool_band[:, GROUP - SEQS - place : 2 * GROUP - SEQS - place],
-                    start=(place == 0),
-                    stop=(place == GROUP - SEQS or block == TENSOR_PIECES * BLOCKS - 1),
+                    start=(g == 0),
+                    stop=(g == PIECES - 1),
                 )
 
-        waiting = flip(look_up(0))
-        for g in range(1, TENSOR_PIECES):
-            flipped = flip(look_up(g))
-            contract(g - 1, waiting)
+        waiting = []
+        g = 0
+        for pieces in LOOK_UPS:
+            err = look_up(g, pieces)
+            flipped = [(g + place, flip(err, place)) for place in range(pieces)]
+            for piece, flipped_piece in waiting:
+                contract(piece, flipped_piece)
             waiting = flipped
-        contract(TENSOR_PIECES - 1, waiting)
-        tensor_seqs = TENSOR_PIECES * PIECE // T
-        nc.scalar.copy(pooled[:, 0:tensor_seqs], pooled_ps[:, 0:tensor_seqs])
+            g += pieces
+        for piece, flipped_piece in waiting:
+            contract(piece, flipped_piece)
 
-        for g in range(TENSOR_PIECES, N // PIECE):
-            err = look_up(g)
-            weighted = flow.tile([D, PIECE // T, T], F32, name="weighted")
-            nc.vector.tensor_tensor(
-                weighted[:],
-                err[:].rearrange("c (b t) -> c b t", t=T),
-                attn[:].unsqueeze(1).to_broadcast([D, PIECE // T, T]),
-                ALU.mult,
-            )
-            nc.vector.reduce_sum(pooled[:, g * (PIECE // T) : (g + 1) * (PIECE // T)], weighted[:], axis=X)
-
-        centered_ps = psum.tile([D, B], F32, name="centered_ps")
-        nc.tensor.matmul(centered_ps[:], center_mat[:], pooled[:], start=True, stop=True)
-        squared = held.tile([D, B], F32, name="squared")
-        nc.scalar.activation(squared[:], centered_ps[:], ACT.Square)
-        var_ps = psum.tile([D, B], F32, name="var_ps")
-        nc.tensor.matmul(var_ps[:], mean_mat[:], squared[:], start=True, stop=True)
-        inv_std = held.tile([D, B], F32, name="inv_std")
-        nc.scalar.activation(inv_std[:], var_ps[:], ACT.Abs_reciprocal_sqrt, bias=eps[:, 0:1])
-        normed = held.tile([D, B], F32, name="normed")
-        nc.vector.tensor_tensor(normed[:], centered_ps[:], inv_std[:], ALU.mult)
+        stats = held.tile([B, 6], F32, name="stats")
+        nc.vector.bn_stats(stats[:], pooled_ps[:])
+        mean_var = held.tile([B, 2], F32, name="mean_var")
+        nc.vector.bn_aggr(mean_var[:], stats[:])
+        inv_std = held.tile([B, 1], F32, name="inv_std")
+        nc.scalar.activation(inv_std[:], mean_var[:, 1:2], ACT.Abs_reciprocal_sqrt, bias=eps[:, 0:1])
+        normed = held.tile([B, D], F32, name="normed")
+        nc.vector.tensor_scalar(
+            normed[:], pooled_ps[:], mean_var[:, 0:1], inv_std[:, 0:1], ALU.subtract, ALU.mult
+        )
+        in_order = held.tile([B, B], F32, name="in_order")
+        nc.gpsimd.tensor_copy(
+            in_order[:].rearrange("p (g i s) -> p g i s", g=PIECES, i=BLOCKS),
+            identity[:].rearrange("p (i g s) -> p g i s", i=BLOCKS, g=PIECES),
+        )
+        back_ps = psum.tile([D, B], F32, name="back_ps")
+        nc.tensor.transpose(back_ps[:], normed[:], in_order[:])
         fn = held.tile([D, B], BF16, name="fn")
-        nc.vector.tensor_scalar(fn[:], normed[:], gain_sb[:, 0:1], shift_sb[:, 0:1], ALU.mult, ALU.add)
+        nc.vector.tensor_scalar(fn[:], back_ps[:], gain_sb[:, 0:1], shift_sb[:, 0:1], ALU.mult, ALU.add)
 
         logits_sb = held.tile([B, V], F32, name="logits_sb")
         for i in range(V // BANK):

@@ -39,12 +39,12 @@ def tile_gdtransformer_kernel(tc, table, kpos, qpos, gain, shift, offs, out):
         nc.scalar.dma_start(kpos_sb[:], kpos)
         qpos_sb = held.tile([D, 1], BF16, name="qpos_sb")
         nc.sync.dma_start(qpos_sb[:], qpos)
-        offsets = held.tile([D, N // 16], U16, name="offsets")
-        nc.sync.dma_start(offsets[:], offs)
         table_sb = held.tile([D, V], F32, name="table_sb")
         for i in range(V // BANK):
             queue = nc.scalar if i % 2 == 0 else nc.sync
             queue.dma_start(table_sb[:, i * BANK : (i + 1) * BANK], table[:, i * BANK : (i + 1) * BANK])
+        offsets = held.tile([D, N // 16], U16, name="offsets")
+        nc.sync.dma_start(offsets[:], offs)
         gain_sb = held.tile([D, 1], F32, name="gain_sb")
         nc.scalar.dma_start(gain_sb[:], gain)
         shift_sb = held.tile([D, 1], F32, name="shift_sb")
@@ -75,20 +75,22 @@ def tile_gdtransformer_kernel(tc, table, kpos, qpos, gain, shift, offs, out):
         nc.vector.reciprocal(inv_sum[:], expo_sum[:])
         attn = held.tile([D, T], F32, name="attn")
         nc.vector.tensor_scalar_mul(attn[:], expo[:], inv_sum[:, 0:1])
-        table_change = held.tile([D, 1], F32, name="table_change")
-        nc.scalar.activation(table_change[:], expo_sum[:], ACT.Abs_reciprocal_sqrt)
-
         table_bf = held.tile([D, V], BF16, name="table_bf")
         chunk_sum = held.tile([D, V // BANK], F32, name="chunk_sum")
         for i in range(V // BANK):
             chunk = table_sb[:, i * BANK : (i + 1) * BANK]
-            nc.vector.reduce_sum(chunk_sum[:, i : i + 1], chunk, axis=X)
-            nc.scalar.copy(table_bf[:, i * BANK : (i + 1) * BANK], chunk)
+            chunk_bf = table_bf[:, i * BANK : (i + 1) * BANK]
+            if i % 2 == 0:
+                nc.scalar.activation(chunk_bf, chunk, ACT.Copy, accum_out=chunk_sum[:, i : i + 1])
+            else:
+                nc.vector.tensor_scalar(chunk_bf, chunk, 1.0, None, ALU.mult, ALU.add, accum_out=chunk_sum[:, i : i + 1])
         table_sum = held.tile([D, 1], F32, name="table_sum")
         nc.vector.reduce_sum(table_sum[:], chunk_sum[:], axis=X)
         minus_mu = held.tile([D, WIDEST], F32, name="minus_mu")
         nc.vector.tensor_scalar_mul(minus_mu[:, 0:PIECE], table_sum[:, 0:1].to_broadcast([D, PIECE]), -1.0 / V)
         nc.scalar.copy(minus_mu[:, PIECE:WIDEST], minus_mu[:, 0:PIECE])
+        table_change = held.tile([D, 1], F32, name="table_change")
+        nc.scalar.activation(table_change[:], minus_mu[:, 0:1], ACT.Abs_reciprocal_sqrt, bias=eps[:, 0:1])
 
         masked = held.tile([BLOCK, SEQS, T], F32, name="masked")
         nc.vector.tensor_tensor(

@@ -113,22 +113,26 @@ def tile_gdtransformer_kernel(tc, table, kpos, qpos, gain, shift, offs, out):
             )
             return err
 
-        def flip(err, place):
+        def flip(err, place, blocks, on_vector):
             flipped_ps = banks.tile([BLOCK, BLOCKS * D], F32, name="flipped_ps", tag="bank")
-            for i in range(BLOCKS):
-                first = place * PIECE + i * BLOCK
+            for i in range(blocks):
+                first = (place + i) * BLOCK
                 nc.tensor.transpose(flipped_ps[:, i * D : (i + 1) * D], err[:, first : first + BLOCK], identity[:])
             flipped = flow.tile([BLOCK, BLOCKS * D], F32, name="flipped")
-            nc.scalar.copy(flipped[:], flipped_ps[:])
+            if on_vector:
+                nc.vector.tensor_copy(flipped[:, 0 : blocks * D], flipped_ps[:, 0 : blocks * D])
+            else:
+                nc.scalar.copy(flipped[:, 0 : blocks * D], flipped_ps[:, 0 : blocks * D])
             return flipped
 
         pooled_ps = psum.tile([B, D], F32, name="pooled_ps")
 
-        def contract(g, flipped):
+        def contract(block, blocks, flipped):
+            g, strip = divmod(block, BLOCKS)
             window = STRIP - SEQS - g * SEQS
-            for i in range(BLOCKS):
+            for i in range(blocks):
                 nc.tensor.matmul(
-                    pooled_ps[i * STRIP : (i + 1) * STRIP, :],
+                    pooled_ps[(strip + i) * STRIP : (strip + i + 1) * STRIP, :],
                     pool_band[:, window : window + STRIP],
                     flipped[:, i * D : (i + 1) * D],
                     start=(g == 0),
@@ -139,13 +143,17 @@ def tile_gdtransformer_kernel(tc, table, kpos, qpos, gain, shift, offs, out):
         g = 0
         for pieces in LOOK_UPS:
             err = look_up(g, pieces)
-            flipped = [(g + place, flip(err, place)) for place in range(pieces)]
-            for piece, flipped_piece in waiting:
-                contract(piece, flipped_piece)
+            in_bank = BLOCKS // 2 if g + pieces == PIECES else BLOCKS
+            flipped = []
+            for place in range(0, pieces * BLOCKS, in_bank):
+                on_vector = in_bank < BLOCKS and place == 0
+                flipped.append((g * BLOCKS + place, in_bank, flip(err, place, in_bank, on_vector)))
+            for waiting_bank in waiting:
+                contract(*waiting_bank)
             waiting = flipped
             g += pieces
-        for piece, flipped_piece in waiting:
-            contract(piece, flipped_piece)
+        for waiting_bank in waiting:
+            contract(*waiting_bank)
 
         stats = held.tile([B, 6], F32, name="stats")
         nc.vector.bn_stats(stats[:], pooled_ps[:])
@@ -168,13 +176,15 @@ def tile_gdtransformer_kernel(tc, table, kpos, qpos, gain, shift, offs, out):
         nc.vector.tensor_scalar(fn[:], back_ps[:], gain_sb[:, 0:1], shift_sb[:, 0:1], ALU.mult, ALU.add)
 
         logits_sb = held.tile([B, V], F32, name="logits_sb")
-        for i in range(V // BANK):
-            words = slice(i * BANK, (i + 1) * BANK)
+        widths = [BANK] * (V // BANK - 1) + [BANK // 2] * 2
+        for i, width in enumerate(widths):
+            first = sum(widths[:i])
+            words = slice(first, first + width)
             logits_ps = banks.tile([B, BANK], F32, name="logits_ps", tag="bank")
-            nc.tensor.matmul(logits_ps[:], fn[:], table_bf[:, words], start=True, stop=True)
+            nc.tensor.matmul(logits_ps[:, 0:width], fn[:], table_bf[:, words], start=True, stop=True)
             if i % 2 == 0:
-                nc.vector.tensor_copy(logits_sb[:, words], logits_ps[:])
+                nc.vector.tensor_copy(logits_sb[:, words], logits_ps[:, 0:width])
                 nc.sync.dma_start(out[:, words], logits_sb[:, words])
             else:
-                nc.scalar.copy(logits_sb[:, words], logits_ps[:])
+                nc.scalar.copy(logits_sb[:, words], logits_ps[:, 0:width])
                 nc.scalar.dma_start(out[:, words], logits_sb[:, words])

@@ -15,11 +15,12 @@ LN_EPS = 1e-5
 BANK = 512
 PIECE = 512
 PIECES = N // PIECE
-LOOK_UPS = (1, 2, 2, 2, 1)
-assert sum(LOOK_UPS) == PIECES
-WIDEST = max(LOOK_UPS) * PIECE
 BLOCK = 128
 BLOCKS = PIECE // BLOCK
+HALF = BLOCKS // 2
+LOOK_UPS = (HALF, HALF, 2 * BLOCKS, 2 * BLOCKS, 2 * BLOCKS, BLOCKS)
+assert sum(LOOK_UPS) == PIECES * BLOCKS
+WIDEST = max(LOOK_UPS) * BLOCK
 SEQS = BLOCK // T
 STRIP = 32
 assert BLOCKS * STRIP == B and PIECES * SEQS == STRIP
@@ -103,12 +104,12 @@ def tile_gdtransformer_kernel(tc, table, kpos, qpos, gain, shift, offs, out):
         nc.gpsimd.memset(pool_band[:], 0.0)
         nc.vector.reduce_sum(pool_band[:, STRIP - SEQS : STRIP], masked[:], axis=X)
 
-        def look_up(g, pieces):
+        def look_up(block, blocks):
             err = flow.tile([D, WIDEST], F32, name="err")
             nc.vector.tensor_tensor(
-                err[:, 0 : pieces * PIECE],
-                table_sb[:].indirect(offsets[:, g * (PIECE // 16) : (g + pieces) * (PIECE // 16)]),
-                minus_mu[:, 0 : pieces * PIECE],
+                err[:, 0 : blocks * BLOCK],
+                table_sb[:].indirect(offsets[:, block * (BLOCK // 16) : (block + blocks) * (BLOCK // 16)]),
+                minus_mu[:, 0 : blocks * BLOCK],
                 ALU.add,
             )
             return err
@@ -140,18 +141,19 @@ def tile_gdtransformer_kernel(tc, table, kpos, qpos, gain, shift, offs, out):
                 )
 
         waiting = []
-        g = 0
-        for pieces in LOOK_UPS:
-            err = look_up(g, pieces)
-            in_bank = BLOCKS // 2 if g + pieces == PIECES else BLOCKS
+        block = 0
+        for blocks in LOOK_UPS:
+            err = look_up(block, blocks)
+            last = block + blocks == PIECES * BLOCKS
+            in_bank = HALF if last else min(blocks, BLOCKS)
             flipped = []
-            for place in range(0, pieces * BLOCKS, in_bank):
-                on_vector = in_bank < BLOCKS and place == 0
-                flipped.append((g * BLOCKS + place, in_bank, flip(err, place, in_bank, on_vector)))
+            for place in range(0, blocks, in_bank):
+                on_vector = last and place == 0
+                flipped.append((block + place, in_bank, flip(err, place, in_bank, on_vector)))
             for waiting_bank in waiting:
                 contract(*waiting_bank)
             waiting = flipped
-            g += pieces
+            block += blocks
         for waiting_bank in waiting:
             contract(*waiting_bank)
 

@@ -21,6 +21,7 @@ HALF = BLOCKS // 2
 LOOK_UPS = (HALF, HALF, 2 * BLOCKS, 2 * BLOCKS, 2 * BLOCKS, BLOCKS)
 assert sum(LOOK_UPS) == PIECES * BLOCKS
 WIDEST = max(LOOK_UPS) * BLOCK
+POOL_FROM = 3
 SEQS = BLOCK // T
 STRIP = 32
 assert BLOCKS * STRIP == B and PIECES * SEQS == STRIP
@@ -32,7 +33,7 @@ def tile_gdtransformer_kernel(tc, table, kpos, qpos, gain, shift, offs, out):
     nc = tc.nc
     with (
         tc.tile_pool(name="held", bufs=1) as held,
-        tc.tile_pool(name="flow", bufs=4) as flow,
+        tc.tile_pool(name="flow", bufs=6) as flow,
         tc.psum_pool(name="psum", bufs=1) as psum,
         tc.psum_pool(name="banks", bufs=4) as banks,
     ):
@@ -51,58 +52,53 @@ def tile_gdtransformer_kernel(tc, table, kpos, qpos, gain, shift, offs, out):
         shift_sb = held.tile([D, 1], F32, name="shift_sb")
         nc.sync.dma_start(shift_sb[:], shift)
 
-        mean_mat = held.tile([D, D], F32, name="mean_mat")
-        nc.vector.memset(mean_mat[:], 1.0 / D)
+        score_mat = held.tile([D, D], F32, name="score_mat")
+        nc.vector.memset(score_mat[:], 1.0 / math.sqrt(D))
         identity = held.tile([D, D], F32, name="identity")
         make_identity(nc, identity[:])
         eps = held.tile([D, 1], F32, name="eps")
         nc.vector.memset(eps[:], LN_EPS)
 
-        qk = held.tile([D, T], F32, name="qk")
-        nc.vector.tensor_scalar_mul(qk[:], kpos_sb[:], qpos_sb[:, 0:1])
-        score_ps = psum.tile([D, T], F32, name="score_ps")
-        nc.tensor.matmul(score_ps[:], mean_mat[:], qk[:], start=True, stop=True)
-        to_score = D / math.sqrt(D)
-        score_max = held.tile([D, 1], F32, name="score_max")
-        nc.vector.reduce_max(score_max[:], score_ps[:], axis=X)
-        minus_max = held.tile([D, 1], F32, name="minus_max")
-        nc.vector.tensor_scalar_mul(minus_max[:], score_max[:], -to_score)
-        expo = held.tile([D, T], F32, name="expo")
-        expo_sum = held.tile([D, 1], F32, name="expo_sum")
-        nc.scalar.activation(
-            expo[:], score_ps[:], ACT.Exp, bias=minus_max[:, 0:1], scale=to_score, accum_out=expo_sum[:, 0:1]
-        )
-        inv_sum = held.tile([D, 1], F32, name="inv_sum")
-        nc.vector.reciprocal(inv_sum[:], expo_sum[:])
-        attn = held.tile([D, T], F32, name="attn")
-        nc.vector.tensor_scalar_mul(attn[:], expo[:], inv_sum[:, 0:1])
-        table_bf = held.tile([D, V], BF16, name="table_bf")
-        chunk_sum = held.tile([D, V // BANK], F32, name="chunk_sum")
-        for i in range(V // BANK):
-            chunk = table_sb[:, i * BANK : (i + 1) * BANK]
-            chunk_bf = table_bf[:, i * BANK : (i + 1) * BANK]
-            if i % 2 == 0:
-                nc.scalar.activation(chunk_bf, chunk, ACT.Copy, accum_out=chunk_sum[:, i : i + 1])
-            else:
-                nc.vector.tensor_scalar(chunk_bf, chunk, 1.0, None, ALU.mult, ALU.add, accum_out=chunk_sum[:, i : i + 1])
-        table_sum = held.tile([D, 1], F32, name="table_sum")
-        nc.vector.reduce_sum(table_sum[:], chunk_sum[:], axis=X)
-        minus_mu = held.tile([D, WIDEST], F32, name="minus_mu")
-        nc.vector.tensor_scalar_mul(minus_mu[:, 0:PIECE], table_sum[:, 0:1].to_broadcast([D, PIECE]), -1.0 / V)
-        nc.scalar.copy(minus_mu[:, PIECE:WIDEST], minus_mu[:, 0:PIECE])
-        table_change = held.tile([D, 1], F32, name="table_change")
-        nc.scalar.activation(table_change[:], minus_mu[:, 0:1], ACT.Abs_reciprocal_sqrt, bias=eps[:, 0:1])
-
-        masked = held.tile([BLOCK, SEQS, T], F32, name="masked")
-        nc.vector.tensor_tensor(
-            masked[:],
-            identity[:].rearrange("j (s t) -> j s t", t=T),
-            attn[:].unsqueeze(1).to_broadcast([BLOCK, SEQS, T]),
-            ALU.mult,
-        )
+        block_mask = held.tile([BLOCK, SEQS], F32, name="block_mask")
+        nc.vector.memset(block_mask[:], 0.0)
+        for s in range(SEQS):
+            nc.vector.memset(block_mask[s * T : (s + 1) * T, s : s + 1], 1.0)
         pool_band = held.tile([BLOCK, 2 * STRIP - SEQS], F32, name="pool_band")
-        nc.gpsimd.memset(pool_band[:], 0.0)
-        nc.vector.reduce_sum(pool_band[:, STRIP - SEQS : STRIP], masked[:], axis=X)
+        nc.vector.memset(pool_band[:], 0.0)
+        qk = held.tile([D, SEQS, T], F32, name="qk")
+        nc.vector.tensor_scalar_mul(qk[:], kpos_sb[:].unsqueeze(1).to_broadcast([D, SEQS, T]), qpos_sb[:, 0:1])
+        score_row_ps = psum.tile([D, T], F32, name="score_row_ps")
+        nc.tensor.matmul(score_row_ps[:], score_mat[:], qk[:, 0, :], start=True, stop=True)
+        score_ps = psum.tile([BLOCK, 1], F32, name="score_ps", tag="late")
+        nc.tensor.matmul(
+            score_ps[:], qk[:].rearrange("c s t -> c (s t)"), score_mat[:, 0:1], start=True, stop=True
+        )
+        minus_max = held.tile([D, 1], F32, name="minus_max")
+        nc.vector.reduce_max(minus_max[:], score_row_ps[:], axis=X, negate=True)
+        expo_row = held.tile([D, T], F32, name="expo_row")
+        expo_sum = held.tile([D, 1], F32, name="expo_sum")
+        nc.scalar.activation(expo_row[:], score_row_ps[:], ACT.Exp, bias=minus_max[:, 0:1], accum_out=expo_sum[:, 0:1])
+        expo = held.tile([BLOCK, 1], F32, name="expo")
+        nc.scalar.activation(expo[:], score_ps[:], ACT.Exp, bias=minus_max[:, 0:1])
+
+        table_bf = held.tile([D, V], BF16, name="table_bf")
+        part_sum = held.tile([D, V // BANK], F32, name="part_sum")
+        for i in range(V // BANK):
+            words = slice(i * BANK, (i + 1) * BANK)
+            row_sum = part_sum[:, i : i + 1]
+            if i % 2 == 0:
+                nc.scalar.activation(table_bf[:, words], table_sb[:, words], ACT.Copy, accum_out=row_sum)
+            else:
+                nc.vector.tensor_scalar(table_bf[:, words], table_sb[:, words], 1.0, None, ALU.mult, ALU.add, accum_out=row_sum)
+        table_sum = held.tile([D, 1], F32, name="table_sum")
+        nc.vector.reduce_sum(table_sum[:], part_sum[:], axis=X)
+        minus_mu = held.tile([D, WIDEST], F32, name="minus_mu")
+        first_cols = HALF * BLOCK
+        nc.vector.tensor_scalar_mul(minus_mu[:, 0:first_cols], table_sum[:, 0:1].to_broadcast([D, first_cols]), -1.0 / V)
+        nc.scalar.mul(minus_mu[:, first_cols:WIDEST], table_sum[:, 0:1].to_broadcast([D, WIDEST - first_cols]), -1.0 / V)
+
+        eps_sum2 = held.tile([D, 1], F32, name="eps_sum2")
+        nc.scalar.activation(eps_sum2[:], expo_sum[:], ACT.Square, scale=math.sqrt(LN_EPS))
 
         def look_up(block, blocks):
             err = flow.tile([D, WIDEST], F32, name="err")
@@ -142,18 +138,25 @@ def tile_gdtransformer_kernel(tc, table, kpos, qpos, gain, shift, offs, out):
 
         waiting = []
         block = 0
-        for blocks in LOOK_UPS:
+        for n, blocks in enumerate(LOOK_UPS):
             err = look_up(block, blocks)
-            last = block + blocks == PIECES * BLOCKS
+            if n == POOL_FROM:
+                nc.vector.tensor_scalar_mul(pool_band[:, STRIP - SEQS : STRIP], block_mask[:], expo[:, 0:1])
+            last = n == len(LOOK_UPS) - 1
             in_bank = HALF if last else min(blocks, BLOCKS)
             flipped = []
             for place in range(0, blocks, in_bank):
                 on_vector = last and place == 0
                 flipped.append((block + place, in_bank, flip(err, place, in_bank, on_vector)))
-            for waiting_bank in waiting:
-                contract(*waiting_bank)
-            waiting = flipped
+            if n >= POOL_FROM:
+                for waiting_bank in waiting:
+                    contract(*waiting_bank)
+                waiting = []
+            waiting += flipped
             block += blocks
+            if block == BLOCKS:
+                table_change = held.tile([BLOCK, 1], F32, name="table_change")
+                nc.scalar.activation(table_change[:], flipped[-1][2][:, 0:1], ACT.Abs_reciprocal_sqrt, bias=eps[:, 0:1])
         for waiting_bank in waiting:
             contract(*waiting_bank)
 
@@ -162,7 +165,7 @@ def tile_gdtransformer_kernel(tc, table, kpos, qpos, gain, shift, offs, out):
         mean_var = held.tile([B, 2], F32, name="mean_var")
         nc.vector.bn_aggr(mean_var[:], stats[:])
         inv_std = held.tile([B, 1], F32, name="inv_std")
-        nc.scalar.activation(inv_std[:], mean_var[:, 1:2], ACT.Abs_reciprocal_sqrt, bias=eps[:, 0:1])
+        nc.scalar.activation(inv_std[:], mean_var[:, 1:2], ACT.Abs_reciprocal_sqrt, bias=eps_sum2[:, 0:1])
         normed = held.tile([B, D], F32, name="normed")
         nc.vector.tensor_scalar(
             normed[:], pooled_ps[:], mean_var[:, 0:1], inv_std[:, 0:1], ALU.subtract, ALU.mult
@@ -172,13 +175,13 @@ def tile_gdtransformer_kernel(tc, table, kpos, qpos, gain, shift, offs, out):
             in_order[:].rearrange("p (g i s) -> p g i s", g=PIECES, i=BLOCKS),
             identity[:].rearrange("p (i g s) -> p g i s", i=BLOCKS, g=PIECES),
         )
-        back_ps = psum.tile([D, B], F32, name="back_ps")
+        back_ps = psum.tile([D, B], F32, name="back_ps", tag="late")
         nc.tensor.transpose(back_ps[:], normed[:], in_order[:])
         fn = held.tile([D, B], BF16, name="fn")
         nc.vector.tensor_scalar(fn[:], back_ps[:], gain_sb[:, 0:1], shift_sb[:, 0:1], ALU.mult, ALU.add)
 
         logits_sb = held.tile([B, V], F32, name="logits_sb")
-        widths = [BANK] * (V // BANK - 1) + [BANK // 2] * 2
+        widths = [BANK // 2] * 2 + [BANK] * (V // BANK - 1)
         for i, width in enumerate(widths):
             first = sum(widths[:i])
             words = slice(first, first + width)
@@ -189,4 +192,4 @@ def tile_gdtransformer_kernel(tc, table, kpos, qpos, gain, shift, offs, out):
                 nc.sync.dma_start(out[:, words], logits_sb[:, words])
             else:
                 nc.scalar.copy(logits_sb[:, words], logits_ps[:, 0:width])
-                nc.scalar.dma_start(out[:, words], logits_sb[:, words])
+                nc.sync.dma_start(out[:, words], logits_sb[:, words])

@@ -18,10 +18,9 @@ PIECES = N // PIECE
 BLOCK = 128
 BLOCKS = PIECE // BLOCK
 HALF = BLOCKS // 2
-LOOK_UPS = (HALF, HALF, 2 * BLOCKS, 2 * BLOCKS, 2 * BLOCKS, BLOCKS)
+LOOK_UPS = (BLOCKS - 1, 2 * BLOCKS + 1, 2 * BLOCKS, 2 * BLOCKS, BLOCKS)
 assert sum(LOOK_UPS) == PIECES * BLOCKS
 WIDEST = max(LOOK_UPS) * BLOCK
-POOL_FROM = 3
 SEQS = BLOCK // T
 STRIP = 32
 assert BLOCKS * STRIP == B and PIECES * SEQS == STRIP
@@ -42,13 +41,18 @@ def tile_gdtransformer_kernel(tc, table, kpos, qpos, gain, shift, offs, out):
         qpos_sb = held.tile([D, 1], BF16, name="qpos_sb")
         nc.sync.dma_start(qpos_sb[:], qpos)
         table_sb = held.tile([D, V], F32, name="table_sb")
-        for i in range(V // BANK):
+        chunks = []
+        for width in (384, 384, 384, 384, 256, 256):
+            first = chunks[-1].stop if chunks else 0
+            chunks.append(slice(first, first + width))
+        assert chunks[-1].stop == V
+        for i, words in enumerate(chunks):
             queue = nc.scalar if i % 2 == 0 else nc.sync
-            queue.dma_start(table_sb[:, i * BANK : (i + 1) * BANK], table[:, i * BANK : (i + 1) * BANK])
+            queue.dma_start(table_sb[:, words], table[:, words])
         offsets = held.tile([D, N // 16], U16, name="offsets")
         nc.sync.dma_start(offsets[:], offs)
         gain_sb = held.tile([D, 1], F32, name="gain_sb")
-        nc.scalar.dma_start(gain_sb[:], gain)
+        nc.sync.dma_start(gain_sb[:], gain)
         shift_sb = held.tile([D, 1], F32, name="shift_sb")
         nc.sync.dma_start(shift_sb[:], shift)
 
@@ -82,21 +86,45 @@ def tile_gdtransformer_kernel(tc, table, kpos, qpos, gain, shift, offs, out):
         nc.scalar.activation(expo[:], score_ps[:], ACT.Exp, bias=minus_max[:, 0:1])
 
         table_bf = held.tile([D, V], BF16, name="table_bf")
-        part_sum = held.tile([D, V // BANK], F32, name="part_sum")
-        for i in range(V // BANK):
-            words = slice(i * BANK, (i + 1) * BANK)
-            row_sum = part_sum[:, i : i + 1]
+        chunk_sum = held.tile([D, len(chunks)], F32, name="chunk_sum")
+        sums = [chunk_sum[:, i : i + 1] for i in range(len(chunks))]
+        for i, words in enumerate(chunks):
             if i % 2 == 0:
-                nc.scalar.activation(table_bf[:, words], table_sb[:, words], ACT.Copy, accum_out=row_sum)
+                nc.scalar.activation(table_bf[:, words], table_sb[:, words], ACT.Copy, scale=-1.0 / V, accum_out=sums[i])
             else:
-                nc.vector.tensor_scalar(table_bf[:, words], table_sb[:, words], 1.0, None, ALU.mult, ALU.add, accum_out=row_sum)
-        table_sum = held.tile([D, 1], F32, name="table_sum")
-        nc.vector.reduce_sum(table_sum[:], part_sum[:], axis=X)
+                nc.vector.tensor_scalar(
+                    table_bf[:, words], table_sb[:, words], -1.0 / V, None, ALU.mult, ALU.add, accum_out=sums[i]
+                )
+        early_sum = held.tile([D, 1], F32, name="early_sum")
+        nc.vector.reduce_sum(early_sum[:], chunk_sum[:, 0 : len(chunks) - 2], axis=X)
         minus_mu = held.tile([D, WIDEST], F32, name="minus_mu")
-        first_cols = HALF * BLOCK
-        nc.vector.tensor_scalar_mul(minus_mu[:, 0:first_cols], table_sum[:, 0:1].to_broadcast([D, first_cols]), -1.0 / V)
-        nc.scalar.mul(minus_mu[:, first_cols:WIDEST], table_sum[:, 0:1].to_broadcast([D, WIDEST - first_cols]), -1.0 / V)
+        first_cols = LOOK_UPS[0] * BLOCK
+        nc.vector.scalar_tensor_tensor(
+            minus_mu[:, 0:first_cols],
+            sums[-1].to_broadcast([D, first_cols]),
+            sums[-2],
+            early_sum[:, 0:1].to_broadcast([D, first_cols]),
+            ALU.add,
+            ALU.add,
+        )
+        other_sums = held.tile([D, 1], F32, name="other_sums")
+        nc.scalar.activation(other_sums[:], sums[-2], ACT.Identity, bias=early_sum[:, 0:1])
+        nc.scalar.activation(
+            minus_mu[:, first_cols:WIDEST],
+            sums[-1].to_broadcast([D, WIDEST - first_cols]),
+            ACT.Identity,
+            bias=other_sums[:, 0:1],
+        )
+        table_change = held.tile([D, 1], F32, name="table_change")
+        nc.scalar.activation(
+            table_change[:], minus_mu[:, WIDEST - 1 : WIDEST], ACT.Abs_reciprocal_sqrt, bias=eps[:, 0:1]
+        )
+        scaled_gain = held.tile([D, 1], F32, name="scaled_gain")
+        nc.gpsimd.tensor_scalar(scaled_gain[:], gain_sb[:], -float(V), None, ALU.mult)
+        scaled_shift = held.tile([D, 1], F32, name="scaled_shift")
+        nc.gpsimd.tensor_scalar(scaled_shift[:], shift_sb[:], -float(V), None, ALU.mult)
 
+        nc.vector.tensor_scalar_mul(pool_band[:, STRIP - SEQS : STRIP], block_mask[:], expo[:, 0:1])
         eps_sum2 = held.tile([D, 1], F32, name="eps_sum2")
         nc.scalar.activation(eps_sum2[:], expo_sum[:], ACT.Square, scale=math.sqrt(LN_EPS))
 
@@ -140,23 +168,18 @@ def tile_gdtransformer_kernel(tc, table, kpos, qpos, gain, shift, offs, out):
         block = 0
         for n, blocks in enumerate(LOOK_UPS):
             err = look_up(block, blocks)
-            if n == POOL_FROM:
-                nc.vector.tensor_scalar_mul(pool_band[:, STRIP - SEQS : STRIP], block_mask[:], expo[:, 0:1])
             last = n == len(LOOK_UPS) - 1
-            in_bank = HALF if last else min(blocks, BLOCKS)
             flipped = []
-            for place in range(0, blocks, in_bank):
+            place = 0
+            while place < blocks:
+                in_bank = HALF if last else min(blocks - place, BLOCKS - (block + place) % BLOCKS)
                 on_vector = last and place == 0
                 flipped.append((block + place, in_bank, flip(err, place, in_bank, on_vector)))
-            if n >= POOL_FROM:
-                for waiting_bank in waiting:
-                    contract(*waiting_bank)
-                waiting = []
-            waiting += flipped
+                place += in_bank
+            for waiting_bank in waiting:
+                contract(*waiting_bank)
+            waiting = flipped
             block += blocks
-            if block == BLOCKS:
-                table_change = held.tile([BLOCK, 1], F32, name="table_change")
-                nc.scalar.activation(table_change[:], flipped[-1][2][:, 0:1], ACT.Abs_reciprocal_sqrt, bias=eps[:, 0:1])
         for waiting_bank in waiting:
             contract(*waiting_bank)
 
@@ -178,7 +201,7 @@ def tile_gdtransformer_kernel(tc, table, kpos, qpos, gain, shift, offs, out):
         back_ps = psum.tile([D, B], F32, name="back_ps", tag="late")
         nc.tensor.transpose(back_ps[:], normed[:], in_order[:])
         fn = held.tile([D, B], BF16, name="fn")
-        nc.vector.tensor_scalar(fn[:], back_ps[:], gain_sb[:, 0:1], shift_sb[:, 0:1], ALU.mult, ALU.add)
+        nc.vector.tensor_scalar(fn[:], back_ps[:], scaled_gain[:, 0:1], scaled_shift[:, 0:1], ALU.mult, ALU.add)
 
         logits_sb = held.tile([B, V], F32, name="logits_sb")
         widths = [BANK // 2] * 2 + [BANK] * (V // BANK - 1)

import math

import concourse.mybir as mybir
from concourse.masks import make_identity

F32 = mybir.dt.float32
BF16 = mybir.dt.bfloat16
U16 = mybir.dt.uint16
ALU = mybir.AluOpType
ACT = mybir.ActivationFunctionType
X = mybir.AxisListType.X

D, V, B, T, N = 128, 2048, 128, 32, 4096
LN_EPS = 1e-5
BANK = 512
PIECE = 512
PIECES = N // PIECE
BLOCK = 128
BLOCKS = PIECE // BLOCK
HALF = BLOCKS // 2
LOOK_UPS = (BLOCKS - 1, 2 * BLOCKS + 1, 2 * BLOCKS, 2 * BLOCKS, BLOCKS)
assert sum(LOOK_UPS) == PIECES * BLOCKS
WIDEST = max(LOOK_UPS) * BLOCK
SEQS = BLOCK // T
STRIP = 32
assert BLOCKS * STRIP == B and PIECES * SEQS == STRIP

FLOPS = 2 * B * D * V + 2 * D * N


def tile_gdtransformer_kernel(tc, table, kpos, qpos, gain, shift, offs, out):
    nc = tc.nc
    with (
        tc.tile_pool(name="held", bufs=1) as held,
        tc.tile_pool(name="flow", bufs=6) as flow,
        tc.psum_pool(name="psum", bufs=1) as psum,
        tc.psum_pool(name="banks", bufs=4) as banks,
    ):
        kpos_sb = held.tile([D, T], BF16, name="kpos_sb")
        nc.scalar.dma_start(kpos_sb[:], kpos)
        qpos_sb = held.tile([D, 1], BF16, name="qpos_sb")
        nc.sync.dma_start(qpos_sb[:], qpos)
        table_sb = held.tile([D, V], F32, name="table_sb")
        chunks = []
        for width in (384, 384, 384, 384, 256, 256):
            first = chunks[-1].stop if chunks else 0
            chunks.append(slice(first, first + width))
        assert chunks[-1].stop == V
        for i, words in enumerate(chunks):
            queue = nc.scalar if i % 2 == 0 else nc.sync
            queue.dma_start(table_sb[:, words], table[:, words])
        offsets = held.tile([D, N // 16], U16, name="offsets")
        nc.sync.dma_start(offsets[:], offs)
        gain_sb = held.tile([D, 1], F32, name="gain_sb")
        nc.sync.dma_start(gain_sb[:], gain)
        shift_sb = held.tile([D, 1], F32, name="shift_sb")
        nc.sync.dma_start(shift_sb[:], shift)

        score_mat = held.tile([D, D], F32, name="score_mat")
        nc.vector.memset(score_mat[:], 1.0 / math.sqrt(D))
        identity = held.tile([D, D], F32, name="identity")
        make_identity(nc, identity[:])
        eps = held.tile([D, 1], F32, name="eps")
        nc.vector.memset(eps[:], LN_EPS)

        block_mask = held.tile([BLOCK, SEQS], F32, name="block_mask")
        nc.vector.memset(block_mask[:], 0.0)
        for s in range(SEQS):
            nc.vector.memset(block_mask[s * T : (s + 1) * T, s : s + 1], 1.0)
        pool_band = held.tile([BLOCK, 2 * STRIP - SEQS], F32, name="pool_band")
        nc.vector.memset(pool_band[:], 0.0)
        qk = held.tile([D, SEQS, T], F32, name="qk")
        nc.vector.tensor_scalar_mul(qk[:], kpos_sb[:].unsqueeze(1).to_broadcast([D, SEQS, T]), qpos_sb[:, 0:1])
        score_row_ps = psum.tile([D, T], F32, name="score_row_ps")
        nc.tensor.matmul(score_row_ps[:], score_mat[:], qk[:, 0, :], start=True, stop=True)
        score_ps = psum.tile([BLOCK, 1], F32, name="score_ps", tag="late")
        nc.tensor.matmul(
            score_ps[:], qk[:].rearrange("c s t -> c (s t)"), score_mat[:, 0:1], start=True, stop=True
        )
        minus_max = held.tile([D, 1], F32, name="minus_max")
        nc.vector.reduce_max(minus_max[:], score_row_ps[:], axis=X, negate=True)
        expo_row = held.tile([D, T], F32, name="expo_row")
        expo_sum = held.tile([D, 1], F32, name="expo_sum")
        nc.scalar.activation(expo_row[:], score_row_ps[:], ACT.Exp, bias=minus_max[:, 0:1], accum_out=expo_sum[:, 0:1])
        expo = held.tile([BLOCK, 1], F32, name="expo")
        nc.scalar.activation(expo[:], score_ps[:], ACT.Exp, bias=minus_max[:, 0:1])

        table_bf = held.tile([D, V], BF16, name="table_bf")
        chunk_sum = held.tile([D, len(chunks)], F32, name="chunk_sum")
        sums = [chunk_sum[:, i : i + 1] for i in range(len(chunks))]
        for i, words in enumerate(chunks):
            if i % 2 == 0:
                nc.scalar.activation(table_bf[:, words], table_sb[:, words], ACT.Copy, scale=-1.0 / V, accum_out=sums[i])
            else:
                nc.vector.tensor_scalar(
                    table_bf[:, words], table_sb[:, words], -1.0 / V, None, ALU.mult, ALU.add, accum_out=sums[i]
                )
        early_sum = held.tile([D, 1], F32, name="early_sum")
        nc.vector.reduce_sum(early_sum[:], chunk_sum[:, 0 : len(chunks) - 2], axis=X)
        minus_mu = held.tile([D, WIDEST], F32, name="minus_mu")
        first_cols = LOOK_UPS[0] * BLOCK
        nc.vector.scalar_tensor_tensor(
            minus_mu[:, 0:first_cols],
            sums[-1].to_broadcast([D, first_cols]),
            sums[-2],
            early_sum[:, 0:1].to_broadcast([D, first_cols]),
            ALU.add,
            ALU.add,
        )
        other_sums = held.tile([D, 1], F32, name="other_sums")
        nc.scalar.activation(other_sums[:], sums[-2], ACT.Identity, bias=early_sum[:, 0:1])
        nc.scalar.activation(
            minus_mu[:, first_cols:WIDEST],
            sums[-1].to_broadcast([D, WIDEST - first_cols]),
            ACT.Identity,
            bias=other_sums[:, 0:1],
        )
        table_change = held.tile([D, 1], F32, name="table_change")
        nc.scalar.activation(
            table_change[:], minus_mu[:, WIDEST - 1 : WIDEST], ACT.Abs_reciprocal_sqrt, bias=eps[:, 0:1]
        )
        scaled_gain = held.tile([D, 1], F32, name="scaled_gain")
        nc.gpsimd.tensor_scalar(scaled_gain[:], gain_sb[:], -float(V), None, ALU.mult)
        scaled_shift = held.tile([D, 1], F32, name="scaled_shift")
        nc.gpsimd.tensor_scalar(scaled_shift[:], shift_sb[:], -float(V), None, ALU.mult)

        nc.vector.tensor_scalar_mul(pool_band[:, STRIP - SEQS : STRIP], block_mask[:], expo[:, 0:1])
        eps_sum2 = held.tile([D, 1], F32, name="eps_sum2")
        nc.scalar.activation(eps_sum2[:], expo_sum[:], ACT.Square, scale=math.sqrt(LN_EPS))

        def look_up(block, blocks):
            err = flow.tile([D, WIDEST], F32, name="err")
            nc.vector.tensor_tensor(
                err[:, 0 : blocks * BLOCK],
                table_sb[:].indirect(offsets[:, block * (BLOCK // 16) : (block + blocks) * (BLOCK // 16)]),
                minus_mu[:, 0 : blocks * BLOCK],
                ALU.add,
            )
            return err

        def flip(err, place, blocks, on_vector):
            flipped_ps = banks.tile([BLOCK, BLOCKS * D], F32, name="flipped_ps", tag="bank")
            for i in range(blocks):
                first = (place + i) * BLOCK
                nc.tensor.transpose(flipped_ps[:, i * D : (i + 1) * D], err[:, first : first + BLOCK], identity[:])
            flipped = flow.tile([BLOCK, BLOCKS * D], F32, name="flipped")
            if on_vector:
                nc.vector.tensor_copy(flipped[:, 0 : blocks * D], flipped_ps[:, 0 : blocks * D])
            else:
                nc.scalar.copy(flipped[:, 0 : blocks * D], flipped_ps[:, 0 : blocks * D])
            return flipped

        pooled_ps = psum.tile([B, D], F32, name="pooled_ps")

        def contract(block, blocks, flipped):
            g, strip = divmod(block, BLOCKS)
            window = STRIP - SEQS - g * SEQS
            for i in range(blocks):
                nc.tensor.matmul(
                    pooled_ps[(strip + i) * STRIP : (strip + i + 1) * STRIP, :],
                    pool_band[:, window : window + STRIP],
                    flipped[:, i * D : (i + 1) * D],
                    start=(g == 0),
                    stop=(g == PIECES - 1),
                )

        waiting = []
        block = 0
        for n, blocks in enumerate(LOOK_UPS):
            err = look_up(block, blocks)
            last = n == len(LOOK_UPS) - 1
            flipped = []
            place = 0
            while place < blocks:
                in_bank = HALF if last else min(blocks - place, BLOCKS - (block + place) % BLOCKS)
                on_vector = last and place == 0
                flipped.append((block + place, in_bank, flip(err, place, in_bank, on_vector)))
                place += in_bank
            for waiting_bank in waiting:
                contract(*waiting_bank)
            waiting = flipped
            block += blocks
        for waiting_bank in waiting:
            contract(*waiting_bank)

        stats = held.tile([B, 6], F32, name="stats")
        nc.vector.bn_stats(stats[:], pooled_ps[:])
        mean_var = held.tile([B, 2], F32, name="mean_var")
        nc.vector.bn_aggr(mean_var[:], stats[:])
        inv_std = held.tile([B, 1], F32, name="inv_std")
        nc.scalar.activation(inv_std[:], mean_var[:, 1:2], ACT.Abs_reciprocal_sqrt, bias=eps_sum2[:, 0:1])
        normed = held.tile([B, D], F32, name="normed")
        nc.vector.tensor_scalar(
            normed[:], pooled_ps[:], mean_var[:, 0:1], inv_std[:, 0:1], ALU.subtract, ALU.mult
        )
        in_order = held.tile([B, B], F32, name="in_order")
        nc.gpsimd.tensor_copy(
            in_order[:].rearrange("p (g i s) -> p g i s", g=PIECES, i=BLOCKS),
            identity[:].rearrange("p (i g s) -> p g i s", i=BLOCKS, g=PIECES),
        )
        back_ps = psum.tile([D, B], F32, name="back_ps", tag="late")
        nc.tensor.transpose(back_ps[:], normed[:], in_order[:])
        fn = held.tile([D, B], BF16, name="fn")
        nc.vector.tensor_scalar(fn[:], back_ps[:], scaled_gain[:, 0:1], scaled_shift[:, 0:1], ALU.mult, ALU.add)

        logits_sb = held.tile([B, V], F32, name="logits_sb")
        widths = [BANK // 2] * 2 + [BANK] * (V // BANK - 1)
        for i, width in enumerate(widths):
            first = sum(widths[:i])
            words = slice(first, first + width)
            logits_ps = banks.tile([B, BANK], F32, name="logits_ps", tag="bank")
            nc.tensor.matmul(logits_ps[:, 0:width], fn[:], table_bf[:, words], start=True, stop=True)
            if i % 2 == 0:
                nc.vector.tensor_copy(logits_sb[:, words], logits_ps[:, 0:width])
                nc.sync.dma_start(out[:, words], logits_sb[:, words])
            else:
                nc.scalar.copy(logits_sb[:, words], logits_ps[:, 0:width])
                nc.sync.dma_start(out[:, words], logits_sb[:, words])
